import numpy as np
import ml_dtypes


def mxq(x, axis, fmt="e4m3"):
    dtype, down = {"e4m3": (ml_dtypes.float8_e4m3fn, 7), "e5m2": (ml_dtypes.float8_e5m2, 14)}[fmt]
    v = np.moveaxis(np.asarray(x, np.float32).astype(ml_dtypes.bfloat16).astype(np.float64), axis, -1)
    blocks = v.reshape(v.shape[:-1] + (-1, 32))
    amax = np.abs(blocks).max(-1, keepdims=True)
    byte = np.maximum(np.where(amax > 0, np.frexp(amax)[1] - 1 + 127, 0) - down, 1)
    scale = np.exp2(byte - 127.0)
    codes = (blocks / scale).astype(np.float32).astype(dtype).astype(np.float64)
    return np.moveaxis((codes * scale).reshape(v.shape), -1, axis)


WIDE = False


def mx_kscale(k):
    if not WIDE:
        return np.ones(k)
    levels = np.array([20, -20, 10, -10, 0])
    a = np.random.permutation(np.resize(levels, k // 512 * 4)).reshape(k // 512, 4)
    idx = np.arange(k)
    return np.exp2(a[idx // 512, idx % 128 // 32])


BF16 = ml_dtypes.bfloat16


def bf(x):
    return np.asarray(x, np.float32).astype(BF16)


def f64(x):
    return np.asarray(x).astype(np.float64)


C, I, T, R, D = 4, 8, 128, 512, 512
N = C * I * T


def sigmoid(v):
    return 1.0 / (1.0 + np.exp(-v))


def setup_inputs():
    s = mx_kscale(N).reshape(C, I, T, 1)
    q0 = bf(np.random.standard_normal((C, I, T, D)) * 0.5)
    c0 = bf(np.random.standard_normal((C, I, T, D)) * 6.0 / np.sqrt(R))
    w_lin = bf(np.random.standard_normal((D + D, D)) * 1.5 / np.sqrt(D))
    b_lin = bf(np.random.standard_normal(D) * 0.2)
    w_gate = bf(np.random.standard_normal((D + D, D)) * 1.5 / np.sqrt(D))
    b_gate = bf(np.random.standard_normal(D) * 0.2)
    g = bf(np.random.standard_normal((C, I, T, D)) * np.exp2(np.random.randint(-12, 1, (C, I, T, 1))) / s)
    cat0 = np.concatenate([f64(q0), f64(c0)], axis=-1)
    upd = np.tanh(cat0 @ f64(w_lin) + f64(b_lin))
    gate = sigmoid(cat0 @ f64(w_gate) + f64(b_gate))
    return {"query": bf(f64(q0) * s), "wc": bf(f64(c0) * s),
            "w_lin": w_lin, "b_lin": b_lin, "w_gate": w_gate, "b_gate": b_gate,
            "upd": np.asarray(upd, np.float32), "gate": np.asarray(gate, np.float32),
            "grad_out": g}


def reference(query, wc, w_lin, b_lin, w_gate, b_gate, upd, gate, grad_out):
    cat = np.concatenate([f64(query), f64(wc)], axis=-1).reshape(N, D + D)
    u = f64(upd).reshape(N, D)
    gt = f64(gate).reshape(N, D)
    dz = f64(grad_out).reshape(N, D) * (1.0 - gt) * (1.0 - u * u)
    return mxq(cat, 0, "e4m3").T @ mxq(dz, 0, "e5m2")

@@ -1,0 +1,159 @@
+from contextlib import ExitStack
+
+import concourse.mybir as mybir
+
+F32 = mybir.dt.float32
+BF16 = mybir.dt.bfloat16
+U32 = mybir.dt.uint32
+U8 = mybir.dt.uint8
+E4M3_X4 = mybir.dt.float8_e4m3fn_x4
+E5M2_X4 = mybir.dt.float8_e5m2_x4
+ALU = mybir.AluOpType
+ACT = mybir.ActivationFunctionType
+
+P = 128
+PACK = 4
+K_PASS = P * PACK
+TOKENS = 4096
+D = 512
+PASSES = TOKENS // K_PASS
+M_TILE = 128
+M_TILES = D // M_TILE
+RUN = 4
+WC_LAG = 2
+
+FLOPS = 2 * TOKENS * (2 * D) * D
+BYTES = TOKENS * D * (2 + 2 + 2 + 4 + 4) + (2 * D) * D * 4
+
+
+def tile_scan_pb_t_v_kernel(
+    tc, query, wc, w_lin, b_lin, w_gate, b_gate, upd, gate, grad_out, out
+):
+    nc = tc.nc
+
+    def by_pass(x):
+        return x.flatten_outer_dims().rearrange("(s p j) d -> s p j d", p=P, j=PACK)
+
+    query_v = by_pass(query)
+    wc_v = by_pass(wc)
+    upd_v = by_pass(upd)
+    gate_v = by_pass(gate)
+    grad_v = by_pass(grad_out)
+
+    with ExitStack() as ctx:
+        raw = ctx.enter_context(tc.tile_pool(name="raw", bufs=4))
+        grouped = ctx.enter_context(tc.tile_pool(name="grouped", bufs=2))
+        codes = ctx.enter_context(tc.tile_pool(name="codes", bufs=3))
+        keep = ctx.enter_context(tc.tile_pool(name="keep", bufs=1))
+        results = ctx.enter_context(tc.tile_pool(name="results", bufs=4))
+        psum = ctx.enter_context(tc.psum_pool(name="psum", bufs=1))
+
+        dz_codes = keep.tile([P, PASSES, D], U32, align_bytes=64)
+        dz_scales = keep.tile([P, PASSES, D], U8, align_bytes=64)
+
+        acc = [psum.tile([M_TILE, D], F32, name="acc%d" % m) for m in range(2 * M_TILES)]
+
+        def regroup(copy, dst, src, cols):
+            copy(
+                out=dst[:, cols, :].rearrange("p (c i) j -> p c j i", i=RUN),
+                in_=src[:, :, cols].rearrange("p j (c i) -> p c j i", i=RUN),
+            )
+
+        def multiply(s, first_bank, cat_codes, cat_scales):
+            for t in range(M_TILES):
+                cols = slice(t * M_TILE, (t + 1) * M_TILE)
+                nc.tensor.matmul_mx(
+                    out=acc[first_bank + t][:],
+                    lhsT=cat_codes[:, cols].bitcast(E4M3_X4),
+                    lhsT_scale=cat_scales[:, cols],
+                    rhs=dz_codes[:, s, :].bitcast(E5M2_X4),
+                    rhs_scale=dz_scales[:, s, :],
+                    start=(s == 0),
+                    stop=(s == PASSES - 1),
+                )
+
+        def store(first_bank):
+            for t in range(M_TILES):
+                m = first_bank + t
+                result = results.tile([M_TILE, D], F32)
+                if m % 2 == 0:
+                    nc.scalar.copy(out=result[:], in_=acc[m][:])
+                else:
+                    nc.vector.tensor_copy(out=result[:], in_=acc[m][:])
+                nc.sync.dma_start(out=out[m * M_TILE : (m + 1) * M_TILE, :], in_=result[:])
+
+        for step in range(PASSES + WC_LAG):
+            s = step
+            r = step - WC_LAG
+            with_dz = s < PASSES
+            with_wc = r >= 0
+
+            if with_dz:
+                upd_raw = raw.tile([P, PACK, D], F32)
+                nc.sync.dma_start(out=upd_raw[:], in_=upd_v[s])
+                gate_raw = raw.tile([P, PACK, D], F32)
+                nc.sync.dma_start(out=gate_raw[:], in_=gate_v[s])
+                grad_raw = raw.tile([P, PACK, D], BF16)
+                nc.sync.dma_start(out=grad_raw[:], in_=grad_v[s])
+                query_raw = raw.tile([P, PACK, D], BF16)
+                nc.sync.dma_start(out=query_raw[:], in_=query_v[s])
+            if with_wc:
+                wc_raw = raw.tile([P, PACK, D], BF16)
+                nc.sync.dma_start(out=wc_raw[:], in_=wc_v[r])
+
+            if with_dz:
+                nc.scalar.activation(out=upd_raw[:], in_=upd_raw[:], func=ACT.Square)
+                nc.vector.scalar_tensor_tensor(
+                    out=gate_raw[:],
+                    in0=gate_raw[:],
+                    scalar=1.0,
+                    in1=grad_raw[:],
+                    op0=ALU.subtract,
+                    op1=ALU.mult,
+                )
+                query_grouped = grouped.tile([P, D, PACK], BF16, align_bytes=64)
+                regroup(nc.scalar.copy, query_grouped, query_raw, slice(0, D))
+                dz_grouped = grouped.tile([P, D, PACK], BF16, align_bytes=64)
+                nc.vector.scalar_tensor_tensor(
+                    out=dz_grouped[:],
+                    in0=upd_raw[:].rearrange("p j w -> p w j"),
+                    scalar=1.0,
+                    in1=gate_raw[:].rearrange("p j w -> p w j"),
+                    op0=ALU.subtract,
+                    op1=ALU.mult,
+                )
+            if with_wc:
+                wc_grouped = grouped.tile([P, D, PACK], BF16, align_bytes=64)
+                if with_dz:
+                    regroup(nc.scalar.copy, wc_grouped, wc_raw, slice(0, D))
+                else:
+                    regroup(nc.scalar.copy, wc_grouped, wc_raw, slice(0, D // 2))
+                    regroup(nc.vector.tensor_copy, wc_grouped, wc_raw, slice(D // 2, D))
+
+            if with_dz:
+                query_codes = codes.tile([P, D], U32, align_bytes=64)
+                query_scales = codes.tile([P, D], U8, align_bytes=64)
+                nc.vector.quantize_mx(
+                    out=query_codes[:].bitcast(E4M3_X4),
+                    scales=query_scales[:],
+                    in_=query_grouped[:].rearrange("p w j -> p (w j)"),
+                )
+                nc.vector.quantize_mx(
+                    out=dz_codes[:, s, :].bitcast(E5M2_X4),
+                    scales=dz_scales[:, s, :],
+                    in_=dz_grouped[:].rearrange("p w j -> p (w j)"),
+                )
+                multiply(s, 0, query_codes, query_scales)
+                if s == PASSES - 1:
+                    store(0)
+            if with_wc:
+                wc_codes = codes.tile([P, D], U32, align_bytes=64)
+                wc_scales = codes.tile([P, D], U8, align_bytes=64)
+                nc.vector.quantize_mx(
+                    out=wc_codes[:].bitcast(E4M3_X4),
+                    scales=wc_scales[:],
+                    in_=wc_grouped[:].rearrange("p w j -> p (w j)"),
+                )
+                multiply(r, M_TILES, wc_codes, wc_scales)
+                if r == PASSES - 1:
+                    store(M_TILES)

@@ -20,7 +20,6 @@ PASSES = TOKENS // K_PASS
 M_TILE = 128
 M_TILES = D // M_TILE
 RUN = 4
-WC_LAG = 2
 
 FLOPS = 2 * TOKENS * (2 * D) * D
 BYTES = TOKENS * D * (2 + 2 + 2 + 4 + 4) + (2 * D) * D * 4
@@ -34,8 +33,7 @@ def tile_scan_pb_t_v_kernel(
     def by_pass(x):
         return x.flatten_outer_dims().rearrange("(s p j) d -> s p j d", p=P, j=PACK)
 
-    query_v = by_pass(query)
-    wc_v = by_pass(wc)
+    cat_v = [by_pass(query), by_pass(wc)]
     upd_v = by_pass(upd)
     gate_v = by_pass(gate)
     grad_v = by_pass(grad_out)
@@ -44,116 +42,85 @@ def tile_scan_pb_t_v_kernel(
         raw = ctx.enter_context(tc.tile_pool(name="raw", bufs=4))
         grouped = ctx.enter_context(tc.tile_pool(name="grouped", bufs=2))
         codes = ctx.enter_context(tc.tile_pool(name="codes", bufs=3))
-        keep = ctx.enter_context(tc.tile_pool(name="keep", bufs=1))
-        results = ctx.enter_context(tc.tile_pool(name="results", bufs=4))
+        results = ctx.enter_context(tc.tile_pool(name="results", bufs=2 * M_TILES))
         psum = ctx.enter_context(tc.psum_pool(name="psum", bufs=1))
-
-        dz_codes = keep.tile([P, PASSES, D], U32, align_bytes=64)
-        dz_scales = keep.tile([P, PASSES, D], U8, align_bytes=64)
 
         acc = [psum.tile([M_TILE, D], F32, name="acc%d" % m) for m in range(2 * M_TILES)]
 
-        def regroup(copy, dst, src, cols):
-            copy(
-                out=dst[:, cols, :].rearrange("p (c i) j -> p c j i", i=RUN),
-                in_=src[:, :, cols].rearrange("p j (c i) -> p c j i", i=RUN),
+        def quantise(values, fmt, name):
+            words = codes.tile([P, D], U32, name=name + "_words", align_bytes=64)
+            scales = codes.tile([P, D], U8, name=name + "_scales", align_bytes=64)
+            nc.vector.quantize_mx(
+                out=words[:].bitcast(fmt),
+                scales=scales[:],
+                in_=values[:].rearrange("p w j -> p (w j)"),
             )
+            return words, scales
 
-        def multiply(s, first_bank, cat_codes, cat_scales):
-            for t in range(M_TILES):
-                cols = slice(t * M_TILE, (t + 1) * M_TILE)
-                nc.tensor.matmul_mx(
-                    out=acc[first_bank + t][:],
-                    lhsT=cat_codes[:, cols].bitcast(E4M3_X4),
-                    lhsT_scale=cat_scales[:, cols],
-                    rhs=dz_codes[:, s, :].bitcast(E5M2_X4),
-                    rhs_scale=dz_scales[:, s, :],
-                    start=(s == 0),
-                    stop=(s == PASSES - 1),
-                )
+        for s in range(PASSES):
+            upd_raw = raw.tile([P, PACK, D], F32)
+            nc.sync.dma_start(out=upd_raw[:], in_=upd_v[s])
+            gate_raw = raw.tile([P, PACK, D], F32)
+            nc.sync.dma_start(out=gate_raw[:], in_=gate_v[s])
+            grad_raw = raw.tile([P, PACK, D], BF16)
+            nc.sync.dma_start(out=grad_raw[:], in_=grad_v[s])
+            cat_raw = []
+            for half in range(2):
+                rows = raw.tile([P, PACK, D], BF16, name="cat_raw%d" % half)
+                nc.sync.dma_start(out=rows[:], in_=cat_v[half][s])
+                cat_raw.append(rows)
 
-        def store(first_bank):
-            for t in range(M_TILES):
-                m = first_bank + t
-                result = results.tile([M_TILE, D], F32)
-                if m % 2 == 0:
-                    nc.scalar.copy(out=result[:], in_=acc[m][:])
-                else:
-                    nc.vector.tensor_copy(out=result[:], in_=acc[m][:])
-                nc.sync.dma_start(out=out[m * M_TILE : (m + 1) * M_TILE, :], in_=result[:])
+            nc.scalar.activation(out=upd_raw[:], in_=upd_raw[:], func=ACT.Square)
+            nc.vector.scalar_tensor_tensor(
+                out=gate_raw[:],
+                in0=gate_raw[:],
+                scalar=1.0,
+                in1=grad_raw[:],
+                op0=ALU.subtract,
+                op1=ALU.mult,
+            )
+            dz_grouped = grouped.tile([P, D, PACK], BF16, align_bytes=64)
+            nc.vector.scalar_tensor_tensor(
+                out=dz_grouped[:],
+                in0=upd_raw[:].rearrange("p j w -> p w j"),
+                scalar=1.0,
+                in1=gate_raw[:].rearrange("p j w -> p w j"),
+                op0=ALU.subtract,
+                op1=ALU.mult,
+            )
+            cat_grouped = []
+            for half in range(2):
+                side_by_side = grouped.tile(
+                    [P, D, PACK], BF16, name="cat_grouped%d" % half, align_bytes=64
+                )
+                nc.scalar.copy(
+                    out=side_by_side[:].rearrange("p (c i) j -> p c j i", i=RUN),
+                    in_=cat_raw[half][:].rearrange("p j (c i) -> p c j i", i=RUN),
+                )
+                cat_grouped.append(side_by_side)
 
-        for step in range(PASSES + WC_LAG):
-            s = step
-            r = step - WC_LAG
-            with_dz = s < PASSES
-            with_wc = r >= 0
+            cat_mx = [quantise(cat_grouped[0], E4M3_X4, "cat0")]
+            dz_words, dz_scales = quantise(dz_grouped, E5M2_X4, "dz")
+            cat_mx.append(quantise(cat_grouped[1], E4M3_X4, "cat1"))
 
-            if with_dz:
-                upd_raw = raw.tile([P, PACK, D], F32)
-                nc.sync.dma_start(out=upd_raw[:], in_=upd_v[s])
-                gate_raw = raw.tile([P, PACK, D], F32)
-                nc.sync.dma_start(out=gate_raw[:], in_=gate_v[s])
-                grad_raw = raw.tile([P, PACK, D], BF16)
-                nc.sync.dma_start(out=grad_raw[:], in_=grad_v[s])
-                query_raw = raw.tile([P, PACK, D], BF16)
-                nc.sync.dma_start(out=query_raw[:], in_=query_v[s])
-            if with_wc:
-                wc_raw = raw.tile([P, PACK, D], BF16)
-                nc.sync.dma_start(out=wc_raw[:], in_=wc_v[r])
+            for half in range(2):
+                cat_words, cat_scales = cat_mx[half]
+                for t in range(M_TILES):
+                    cols = slice(t * M_TILE, (t + 1) * M_TILE)
+                    nc.tensor.matmul_mx(
+                        out=acc[half * M_TILES + t][:],
+                        lhsT=cat_words[:, cols].bitcast(E4M3_X4),
+                        lhsT_scale=cat_scales[:, cols],
+                        rhs=dz_words[:].bitcast(E5M2_X4),
+                        rhs_scale=dz_scales[:],
+                        start=(s == 0),
+                        stop=(s == PASSES - 1),
+                    )
 
-            if with_dz:
-                nc.scalar.activation(out=upd_raw[:], in_=upd_raw[:], func=ACT.Square)
-                nc.vector.scalar_tensor_tensor(
-                    out=gate_raw[:],
-                    in0=gate_raw[:],
-                    scalar=1.0,
-                    in1=grad_raw[:],
-                    op0=ALU.subtract,
-                    op1=ALU.mult,
-                )
-                query_grouped = grouped.tile([P, D, PACK], BF16, align_bytes=64)
-                regroup(nc.scalar.copy, query_grouped, query_raw, slice(0, D))
-                dz_grouped = grouped.tile([P, D, PACK], BF16, align_bytes=64)
-                nc.vector.scalar_tensor_tensor(
-                    out=dz_grouped[:],
-                    in0=upd_raw[:].rearrange("p j w -> p w j"),
-                    scalar=1.0,
-                    in1=gate_raw[:].rearrange("p j w -> p w j"),
-                    op0=ALU.subtract,
-                    op1=ALU.mult,
-                )
-            if with_wc:
-                wc_grouped = grouped.tile([P, D, PACK], BF16, align_bytes=64)
-                if with_dz:
-                    regroup(nc.scalar.copy, wc_grouped, wc_raw, slice(0, D))
-                else:
-                    regroup(nc.scalar.copy, wc_grouped, wc_raw, slice(0, D // 2))
-                    regroup(nc.vector.tensor_copy, wc_grouped, wc_raw, slice(D // 2, D))
-
-            if with_dz:
-                query_codes = codes.tile([P, D], U32, align_bytes=64)
-                query_scales = codes.tile([P, D], U8, align_bytes=64)
-                nc.vector.quantize_mx(
-                    out=query_codes[:].bitcast(E4M3_X4),
-                    scales=query_scales[:],
-                    in_=query_grouped[:].rearrange("p w j -> p (w j)"),
-                )
-                nc.vector.quantize_mx(
-                    out=dz_codes[:, s, :].bitcast(E5M2_X4),
-                    scales=dz_scales[:, s, :],
-                    in_=dz_grouped[:].rearrange("p w j -> p (w j)"),
-                )
-                multiply(s, 0, query_codes, query_scales)
-                if s == PASSES - 1:
-                    store(0)
-            if with_wc:
-                wc_codes = codes.tile([P, D], U32, align_bytes=64)
-                wc_scales = codes.tile([P, D], U8, align_bytes=64)
-                nc.vector.quantize_mx(
-                    out=wc_codes[:].bitcast(E4M3_X4),
-                    scales=wc_scales[:],
-                    in_=wc_grouped[:].rearrange("p w j -> p (w j)"),
-                )
-                multiply(r, M_TILES, wc_codes, wc_scales)
-                if r == PASSES - 1:
-                    store(M_TILES)
+        for m in range(2 * M_TILES):
+            result = results.tile([M_TILE, D], F32)
+            if m % 2 == 0:
+                nc.scalar.copy(out=result[:], in_=acc[m][:])
+            else:
+                nc.vector.tensor_copy(out=result[:], in_=acc[m][:])
+            nc.sync.dma_start(out=out[m * M_TILE : (m + 1) * M_TILE, :], in_=result[:])

@@ -33,10 +33,13 @@ def tile_scan_pb_t_v_kernel(
     def by_pass(x):
         return x.flatten_outer_dims().rearrange("(s p j) d -> s p j d", p=P, j=PACK)
 
-    cat_v = [by_pass(query), by_pass(wc)]
-    upd_v = by_pass(upd)
-    gate_v = by_pass(gate)
-    grad_v = by_pass(grad_out)
+    sources = {
+        "upd": (by_pass(upd), F32),
+        "gate": (by_pass(gate), F32),
+        "grad": (by_pass(grad_out), BF16),
+        "query": (by_pass(query), BF16),
+        "wc": (by_pass(wc), BF16),
+    }
 
     with ExitStack() as ctx:
         raw = ctx.enter_context(tc.tile_pool(name="raw", bufs=4))
@@ -57,70 +60,141 @@ def tile_scan_pb_t_v_kernel(
             )
             return words, scales
 
-        for s in range(PASSES):
-            upd_raw = raw.tile([P, PACK, D], F32)
-            nc.sync.dma_start(out=upd_raw[:], in_=upd_v[s])
-            gate_raw = raw.tile([P, PACK, D], F32)
-            nc.sync.dma_start(out=gate_raw[:], in_=gate_v[s])
-            grad_raw = raw.tile([P, PACK, D], BF16)
-            nc.sync.dma_start(out=grad_raw[:], in_=grad_v[s])
-            cat_raw = []
-            for half in range(2):
-                rows = raw.tile([P, PACK, D], BF16, name="cat_raw%d" % half)
-                nc.sync.dma_start(out=rows[:], in_=cat_v[half][s])
-                cat_raw.append(rows)
+        tiles = {}
 
-            nc.scalar.activation(out=upd_raw[:], in_=upd_raw[:], func=ACT.Square)
+        def load(name, s):
+            view, dtype = sources[name]
+            rows = raw.tile([P, PACK, D], dtype, name=name + "_raw")
+            nc.sync.dma_start(out=rows[:], in_=view[s])
+            tiles[(name, s)] = rows
+
+        def square(s, parts):
+            upd_raw = tiles[("upd", s)]
+            for part in range(parts):
+                cols = slice(part * (D // parts), (part + 1) * (D // parts))
+                nc.scalar.activation(
+                    out=upd_raw[:, :, cols], in_=upd_raw[:, :, cols], func=ACT.Square
+                )
+
+        def gate_times_grad(s):
+            gate_raw = tiles[("gate", s)]
             nc.vector.scalar_tensor_tensor(
                 out=gate_raw[:],
                 in0=gate_raw[:],
                 scalar=1.0,
-                in1=grad_raw[:],
+                in1=tiles[("grad", s)][:],
                 op0=ALU.subtract,
                 op1=ALU.mult,
             )
+
+        def dz_product(s, parts):
             dz_grouped = grouped.tile([P, D, PACK], BF16, align_bytes=64)
-            nc.vector.scalar_tensor_tensor(
-                out=dz_grouped[:],
-                in0=upd_raw[:].rearrange("p j w -> p w j"),
-                scalar=1.0,
-                in1=gate_raw[:].rearrange("p j w -> p w j"),
-                op0=ALU.subtract,
-                op1=ALU.mult,
-            )
-            cat_grouped = []
-            for half in range(2):
-                side_by_side = grouped.tile(
-                    [P, D, PACK], BF16, name="cat_grouped%d" % half, align_bytes=64
+            for part in range(parts):
+                cols = slice(part * (D // parts), (part + 1) * (D // parts))
+                nc.vector.scalar_tensor_tensor(
+                    out=dz_grouped[:, cols, :],
+                    in0=tiles[("upd", s)][:, :, cols].rearrange("p j w -> p w j"),
+                    scalar=1.0,
+                    in1=tiles[("gate", s)][:, :, cols].rearrange("p j w -> p w j"),
+                    op0=ALU.subtract,
+                    op1=ALU.mult,
                 )
+            tiles[("dz_grouped", s)] = dz_grouped
+
+        def regroup(name, s, cols=slice(0, D), on_vector=False):
+            if (name + "_grouped", s) not in tiles:
+                tiles[(name + "_grouped", s)] = grouped.tile(
+                    [P, D, PACK], BF16, name=name + "_grouped", align_bytes=64
+                )
+            side_by_side = tiles[(name + "_grouped", s)]
+            if on_vector:
+                nc.vector.tensor_copy(
+                    out=side_by_side[:, cols, :],
+                    in_=tiles[(name, s)][:, :, cols].rearrange("p j w -> p w j"),
+                )
+            else:
                 nc.scalar.copy(
-                    out=side_by_side[:].rearrange("p (c i) j -> p c j i", i=RUN),
-                    in_=cat_raw[half][:].rearrange("p j (c i) -> p c j i", i=RUN),
+                    out=side_by_side[:, cols, :].rearrange("p (c i) j -> p c j i", i=RUN),
+                    in_=tiles[(name, s)][:, :, cols].rearrange("p j (c i) -> p c j i", i=RUN),
                 )
-                cat_grouped.append(side_by_side)
 
-            cat_mx = [quantise(cat_grouped[0], E4M3_X4, "cat0")]
-            dz_words, dz_scales = quantise(dz_grouped, E5M2_X4, "dz")
-            cat_mx.append(quantise(cat_grouped[1], E4M3_X4, "cat1"))
+        def quantise_pass(name, s, cols=slice(0, D)):
+            fmt = E5M2_X4 if name == "dz" else E4M3_X4
+            if (name + "_mx", s) not in tiles:
+                tiles[(name + "_mx", s)] = (
+                    codes.tile([P, D], U32, name=name + "_words", align_bytes=64),
+                    codes.tile([P, D], U8, name=name + "_scales", align_bytes=64),
+                )
+            words, scales = tiles[(name + "_mx", s)]
+            nc.vector.quantize_mx(
+                out=words[:, cols].bitcast(fmt),
+                scales=scales[:, cols],
+                in_=tiles[(name + "_grouped", s)][:, cols, :].rearrange("p w j -> p (w j)"),
+            )
 
-            for half in range(2):
-                cat_words, cat_scales = cat_mx[half]
-                for t in range(M_TILES):
-                    cols = slice(t * M_TILE, (t + 1) * M_TILE)
-                    nc.tensor.matmul_mx(
-                        out=acc[half * M_TILES + t][:],
-                        lhsT=cat_words[:, cols].bitcast(E4M3_X4),
-                        lhsT_scale=cat_scales[:, cols],
-                        rhs=dz_words[:].bitcast(E5M2_X4),
-                        rhs_scale=dz_scales[:],
-                        start=(s == 0),
-                        stop=(s == PASSES - 1),
-                    )
+        def multiply(name, s, m_tiles=(0, 1, 2, 3)):
+            cat_words, cat_scales = tiles[(name + "_mx", s)]
+            dz_words, dz_scales = tiles[("dz_mx", s)]
+            first_bank = 0 if name == "query" else M_TILES
+            for t in m_tiles:
+                cols = slice(t * M_TILE, (t + 1) * M_TILE)
+                nc.tensor.matmul_mx(
+                    out=acc[first_bank + t][:],
+                    lhsT=cat_words[:, cols].bitcast(E4M3_X4),
+                    lhsT_scale=cat_scales[:, cols],
+                    rhs=dz_words[:].bitcast(E5M2_X4),
+                    rhs_scale=dz_scales[:],
+                    start=(s == 0),
+                    stop=(s == PASSES - 1),
+                )
 
-        for m in range(2 * M_TILES):
+        def empty(m, engine):
             result = results.tile([M_TILE, D], F32)
-            if m % 2 == 0:
+            if engine == "scalar":
                 nc.scalar.copy(out=result[:], in_=acc[m][:])
             else:
                 nc.vector.tensor_copy(out=result[:], in_=acc[m][:])
             nc.sync.dma_start(out=out[m * M_TILE : (m + 1) * M_TILE, :], in_=result[:])
+
+        for s in range(PASSES - 2):
+            for name in ("upd", "gate", "grad", "query", "wc"):
+                load(name, s)
+            square(s, 1)
+            gate_times_grad(s)
+            dz_product(s, 1)
+            regroup("query", s)
+            regroup("wc", s)
+            quantise_pass("query", s)
+            quantise_pass("dz", s)
+            quantise_pass("wc", s)
+            multiply("query", s)
+            multiply("wc", s)
+
+        a, b = PASSES - 2, PASSES - 1
+        for s in (a, b):
+            for name in ("upd", "gate", "grad", "query"):
+                load(name, s)
+        load("wc", a)
+        load("wc", b)
+        for s in (a, b):
+            square(s, 1)
+            gate_times_grad(s)
+            dz_product(s, 1)
+            regroup("query", s)
+            quantise_pass("query", s)
+            quantise_pass("dz", s)
+            multiply("query", s)
+        regroup("wc", a)
+        quantise_pass("wc", a)
+        multiply("wc", a)
+        empty(0, "vector")
+        empty(1, "vector")
+        regroup("wc", b)
+        quantise_pass("wc", b)
+        multiply("wc", b)
+        empty(2, "scalar")
+        empty(3, "scalar")
+        empty(4, "vector")
+        empty(5, "scalar")
+        empty(6, "vector")
+        empty(7, "scalar")

@@ -19,6 +19,7 @@ D = 512
 PASSES = TOKENS // K_PASS
 M_TILE = 128
 M_TILES = D // M_TILE
+HELD = 3
 RUN = 4
 
 FLOPS = 2 * TOKENS * (2 * D) * D
@@ -45,6 +46,7 @@ def tile_scan_pb_t_v_kernel(
         raw = ctx.enter_context(tc.tile_pool(name="raw", bufs=4))
         grouped = ctx.enter_context(tc.tile_pool(name="grouped", bufs=2))
         codes = ctx.enter_context(tc.tile_pool(name="codes", bufs=3))
+        dz_codes = ctx.enter_context(tc.tile_pool(name="dz_codes", bufs=HELD + 2))
         results = ctx.enter_context(tc.tile_pool(name="results", bufs=2 * M_TILES))
         psum = ctx.enter_context(tc.psum_pool(name="psum", bufs=1))
 
@@ -60,6 +62,7 @@ def tile_scan_pb_t_v_kernel(
             )
             return words, scales
 
+        ctx.enter_context(tc.manual_schedule(engines={mybir.EngineType.PE}))
         tiles = {}
 
         def load(name, s):
@@ -121,9 +124,10 @@ def tile_scan_pb_t_v_kernel(
         def quantise_pass(name, s, cols=slice(0, D)):
             fmt = E5M2_X4 if name == "dz" else E4M3_X4
             if (name + "_mx", s) not in tiles:
+                pool = dz_codes if name == "dz" else codes
                 tiles[(name + "_mx", s)] = (
-                    codes.tile([P, D], U32, name=name + "_words", align_bytes=64),
-                    codes.tile([P, D], U8, name=name + "_scales", align_bytes=64),
+                    pool.tile([P, D], U32, name=name + "_words", align_bytes=64),
+                    pool.tile([P, D], U8, name=name + "_scales", align_bytes=64),
                 )
             words, scales = tiles[(name + "_mx", s)]
             nc.vector.quantize_mx(
@@ -168,7 +172,8 @@ def tile_scan_pb_t_v_kernel(
             quantise_pass("dz", s)
             quantise_pass("wc", s)
             multiply("query", s)
-            multiply("wc", s)
+            if s < PASSES - 2 - HELD:
+                multiply("wc", s)
 
         a, b = PASSES - 2, PASSES - 1
         for s in (a, b):
@@ -184,6 +189,9 @@ def tile_scan_pb_t_v_kernel(
             quantise_pass("query", s)
             quantise_pass("dz", s)
             multiply("query", s)
+            if s == a:
+                for held in range(PASSES - 2 - HELD, PASSES - 2):
+                    multiply("wc", held)
         regroup("wc", a)
         quantise_pass("wc", a)
         multiply("wc", a)

@@ -19,7 +19,8 @@ D = 512
 PASSES = TOKENS // K_PASS
 M_TILE = 128
 M_TILES = D // M_TILE
-HELD = 3
+LATE = 2
+HELD = 4
 RUN = 4
 
 FLOPS = 2 * TOKENS * (2 * D) * D
@@ -45,8 +46,8 @@ def tile_scan_pb_t_v_kernel(
     with ExitStack() as ctx:
         raw = ctx.enter_context(tc.tile_pool(name="raw", bufs=4))
         grouped = ctx.enter_context(tc.tile_pool(name="grouped", bufs=2))
-        codes = ctx.enter_context(tc.tile_pool(name="codes", bufs=3))
-        dz_codes = ctx.enter_context(tc.tile_pool(name="dz_codes", bufs=HELD + 2))
+        codes = ctx.enter_context(tc.tile_pool(name="codes", bufs=max(3, HELD)))
+        dz_codes = ctx.enter_context(tc.tile_pool(name="dz_codes", bufs=HELD + LATE))
         results = ctx.enter_context(tc.tile_pool(name="results", bufs=2 * M_TILES))
         psum = ctx.enter_context(tc.psum_pool(name="psum", bufs=1))
 
@@ -160,7 +161,8 @@ def tile_scan_pb_t_v_kernel(
                 nc.vector.tensor_copy(out=result[:], in_=acc[m][:])
             nc.sync.dma_start(out=out[m * M_TILE : (m + 1) * M_TILE, :], in_=result[:])
 
-        for s in range(PASSES - 2):
+        early = PASSES - LATE
+        for s in range(early):
             for name in ("upd", "gate", "grad", "query", "wc"):
                 load(name, s)
             square(s, 1)
@@ -172,16 +174,15 @@ def tile_scan_pb_t_v_kernel(
             quantise_pass("dz", s)
             quantise_pass("wc", s)
             multiply("query", s)
-            if s < PASSES - 2 - HELD:
+            if s < early - HELD:
                 multiply("wc", s)
 
-        a, b = PASSES - 2, PASSES - 1
-        for s in (a, b):
+        for s in range(early, PASSES):
             for name in ("upd", "gate", "grad", "query"):
                 load(name, s)
-        load("wc", a)
-        load("wc", b)
-        for s in (a, b):
+        for s in range(early, PASSES):
+            load("wc", s)
+        for s in range(early, PASSES):
             square(s, 1)
             gate_times_grad(s)
             dz_product(s, 1)
@@ -189,17 +190,16 @@ def tile_scan_pb_t_v_kernel(
             quantise_pass("query", s)
             quantise_pass("dz", s)
             multiply("query", s)
-            if s == a:
-                for held in range(PASSES - 2 - HELD, PASSES - 2):
+            if s == PASSES - 2:
+                for held in range(early - HELD, early):
                     multiply("wc", held)
-        regroup("wc", a)
-        quantise_pass("wc", a)
-        multiply("wc", a)
-        empty(0, "vector")
-        empty(1, "vector")
-        regroup("wc", b)
-        quantise_pass("wc", b)
-        multiply("wc", b)
+        for s in range(early, PASSES):
+            regroup("wc", s)
+            quantise_pass("wc", s)
+            multiply("wc", s)
+            if s == PASSES - 2:
+                empty(0, "vector")
+                empty(1, "vector")
         empty(2, "scalar")
         empty(3, "scalar")
         empty(4, "vector")

from contextlib import ExitStack

import concourse.mybir as mybir

F32 = mybir.dt.float32
BF16 = mybir.dt.bfloat16
U32 = mybir.dt.uint32
U8 = mybir.dt.uint8
E4M3_X4 = mybir.dt.float8_e4m3fn_x4
E5M2_X4 = mybir.dt.float8_e5m2_x4
ALU = mybir.AluOpType
ACT = mybir.ActivationFunctionType

P = 128
PACK = 4
K_PASS = P * PACK
TOKENS = 4096
D = 512
PASSES = TOKENS // K_PASS
M_TILE = 128
M_TILES = D // M_TILE
LATE = 2
HELD = 4
RUN = 4

FLOPS = 2 * TOKENS * (2 * D) * D
BYTES = TOKENS * D * (2 + 2 + 2 + 4 + 4) + (2 * D) * D * 4


def tile_scan_pb_t_v_kernel(
    tc, query, wc, w_lin, b_lin, w_gate, b_gate, upd, gate, grad_out, out
):
    nc = tc.nc

    def by_pass(x):
        return x.flatten_outer_dims().rearrange("(s p j) d -> s p j d", p=P, j=PACK)

    sources = {
        "upd": (by_pass(upd), F32),
        "gate": (by_pass(gate), F32),
        "grad": (by_pass(grad_out), BF16),
        "query": (by_pass(query), BF16),
        "wc": (by_pass(wc), BF16),
    }

    with ExitStack() as ctx:
        raw = ctx.enter_context(tc.tile_pool(name="raw", bufs=4))
        grouped = ctx.enter_context(tc.tile_pool(name="grouped", bufs=2))
        codes = ctx.enter_context(tc.tile_pool(name="codes", bufs=max(3, HELD)))
        dz_codes = ctx.enter_context(tc.tile_pool(name="dz_codes", bufs=HELD + LATE))
        results = ctx.enter_context(tc.tile_pool(name="results", bufs=2 * M_TILES))
        psum = ctx.enter_context(tc.psum_pool(name="psum", bufs=1))

        acc = [psum.tile([M_TILE, D], F32, name="acc%d" % m) for m in range(2 * M_TILES)]

        def quantise(values, fmt, name):
            words = codes.tile([P, D], U32, name=name + "_words", align_bytes=64)
            scales = codes.tile([P, D], U8, name=name + "_scales", align_bytes=64)
            nc.vector.quantize_mx(
                out=words[:].bitcast(fmt),
                scales=scales[:],
                in_=values[:].rearrange("p w j -> p (w j)"),
            )
            return words, scales

        ctx.enter_context(tc.manual_schedule(engines={mybir.EngineType.PE}))
        tiles = {}

        def load(name, s):
            view, dtype = sources[name]
            rows = raw.tile([P, PACK, D], dtype, name=name + "_raw")
            nc.sync.dma_start(out=rows[:], in_=view[s])
            tiles[(name, s)] = rows

        def square(s, parts):
            upd_raw = tiles[("upd", s)]
            for part in range(parts):
                cols = slice(part * (D // parts), (part + 1) * (D // parts))
                nc.scalar.activation(
                    out=upd_raw[:, :, cols], in_=upd_raw[:, :, cols], func=ACT.Square
                )

        def gate_times_grad(s):
            gate_raw = tiles[("gate", s)]
            nc.vector.scalar_tensor_tensor(
                out=gate_raw[:],
                in0=gate_raw[:],
                scalar=1.0,
                in1=tiles[("grad", s)][:],
                op0=ALU.subtract,
                op1=ALU.mult,
            )

        def dz_product(s, parts):
            dz_grouped = grouped.tile([P, D, PACK], BF16, align_bytes=64)
            for part in range(parts):
                cols = slice(part * (D // parts), (part + 1) * (D // parts))
                nc.vector.scalar_tensor_tensor(
                    out=dz_grouped[:, cols, :],
                    in0=tiles[("upd", s)][:, :, cols].rearrange("p j w -> p w j"),
                    scalar=1.0,
                    in1=tiles[("gate", s)][:, :, cols].rearrange("p j w -> p w j"),
                    op0=ALU.subtract,
                    op1=ALU.mult,
                )
            tiles[("dz_grouped", s)] = dz_grouped

        def regroup(name, s, cols=slice(0, D), on_vector=False):
            if (name + "_grouped", s) not in tiles:
                tiles[(name + "_grouped", s)] = grouped.tile(
                    [P, D, PACK], BF16, name=name + "_grouped", align_bytes=64
                )
            side_by_side = tiles[(name + "_grouped", s)]
            if on_vector:
                nc.vector.tensor_copy(
                    out=side_by_side[:, cols, :],
                    in_=tiles[(name, s)][:, :, cols].rearrange("p j w -> p w j"),
                )
            else:
                nc.scalar.copy(
                    out=side_by_side[:, cols, :].rearrange("p (c i) j -> p c j i", i=RUN),
                    in_=tiles[(name, s)][:, :, cols].rearrange("p j (c i) -> p c j i", i=RUN),
                )

        def quantise_pass(name, s, cols=slice(0, D)):
            fmt = E5M2_X4 if name == "dz" else E4M3_X4
            if (name + "_mx", s) not in tiles:
                pool = dz_codes if name == "dz" else codes
                tiles[(name + "_mx", s)] = (
                    pool.tile([P, D], U32, name=name + "_words", align_bytes=64),
                    pool.tile([P, D], U8, name=name + "_scales", align_bytes=64),
                )
            words, scales = tiles[(name + "_mx", s)]
            nc.vector.quantize_mx(
                out=words[:, cols].bitcast(fmt),
                scales=scales[:, cols],
                in_=tiles[(name + "_grouped", s)][:, cols, :].rearrange("p w j -> p (w j)"),
            )

        def multiply(name, s, m_tiles=(0, 1, 2, 3)):
            cat_words, cat_scales = tiles[(name + "_mx", s)]
            dz_words, dz_scales = tiles[("dz_mx", s)]
            first_bank = 0 if name == "query" else M_TILES
            for t in m_tiles:
                cols = slice(t * M_TILE, (t + 1) * M_TILE)
                nc.tensor.matmul_mx(
                    out=acc[first_bank + t][:],
                    lhsT=cat_words[:, cols].bitcast(E4M3_X4),
                    lhsT_scale=cat_scales[:, cols],
                    rhs=dz_words[:].bitcast(E5M2_X4),
                    rhs_scale=dz_scales[:],
                    start=(s == 0),
                    stop=(s == PASSES - 1),
                )

        def empty(m, engine):
            result = results.tile([M_TILE, D], F32)
            if engine == "scalar":
                nc.scalar.copy(out=result[:], in_=acc[m][:])
            else:
                nc.vector.tensor_copy(out=result[:], in_=acc[m][:])
            nc.sync.dma_start(out=out[m * M_TILE : (m + 1) * M_TILE, :], in_=result[:])

        early = PASSES - LATE
        for s in range(early):
            for name in ("upd", "gate", "grad", "query", "wc"):
                load(name, s)
            square(s, 1)
            gate_times_grad(s)
            dz_product(s, 1)
            regroup("query", s)
            regroup("wc", s)
            quantise_pass("query", s)
            quantise_pass("dz", s)
            quantise_pass("wc", s)
            multiply("query", s)
            if s < early - HELD:
                multiply("wc", s)

        for s in range(early, PASSES):
            for name in ("upd", "gate", "grad", "query"):
                load(name, s)
        for s in range(early, PASSES):
            load("wc", s)
        for s in range(early, PASSES):
            square(s, 1)
            gate_times_grad(s)
            dz_product(s, 1)
            regroup("query", s)
            quantise_pass("query", s)
            quantise_pass("dz", s)
            multiply("query", s)
            if s == PASSES - 2:
                for held in range(early - HELD, early):
                    multiply("wc", held)
        for s in range(early, PASSES):
            regroup("wc", s)
            quantise_pass("wc", s)
            multiply("wc", s)
            if s == PASSES - 2:
                empty(0, "vector")
                empty(1, "vector")
        empty(2, "scalar")
        empty(3, "scalar")
        empty(4, "vector")
        empty(5, "scalar")
        empty(6, "vector")
        empty(7, "scalar")
